import numpy as np
import ml_dtypes


def mxq(x, axis, fmt="e4m3"):
    dtype, down = {"e4m3": (ml_dtypes.float8_e4m3fn, 7), "e5m2": (ml_dtypes.float8_e5m2, 14)}[fmt]
    v = np.moveaxis(np.asarray(x, np.float32).astype(ml_dtypes.bfloat16).astype(np.float64), axis, -1)
    blocks = v.reshape(v.shape[:-1] + (-1, 32))
    amax = np.abs(blocks).max(-1, keepdims=True)
    byte = np.maximum(np.where(amax > 0, np.frexp(amax)[1] - 1 + 127, 0) - down, 1)
    scale = np.exp2(byte - 127.0)
    codes = (blocks / scale).astype(np.float32).astype(dtype).astype(np.float64)
    return np.moveaxis((codes * scale).reshape(v.shape), -1, axis)


WIDE = False


def mx_kscale(k):
    if not WIDE:
        return np.ones(k)
    levels = np.array([30, -30])
    if k % 512:
        return np.exp2(np.random.permutation(np.resize(levels, k // 32))).repeat(32)
    a = np.empty((k // 512, 16))
    for p in range(k // 512):
        a[p, :8] = np.random.permutation(np.resize(levels, 8))
        for g in range(8):
            far = levels[np.abs(levels - a[p, g]) >= 10]
            a[p, g + 8] = far[np.random.randint(len(far))]
    return np.exp2(a.ravel()).repeat(32)


BF16 = ml_dtypes.bfloat16


def bf(x):
    return np.asarray(x, np.float32).astype(BF16)


def f64(x):
    return np.asarray(x).astype(np.float64)


E, T, H, D, R = 4, 256, 1024, 1024, 128
SCALE = 2.0


def setup_inputs():
    s = mx_kscale(D)
    return {"h": bf(np.random.standard_normal((E, T, D)) * 0.8 * s),
            "low_d": bf(np.random.standard_normal((E, T, R)) * 1.2),
            "W_d": bf(np.random.standard_normal((E, H, D)) * 1.5 / np.sqrt(D) / s),
            "B_d": bf(np.random.standard_normal((E, H, R)) * 0.3 / np.sqrt(R))}


def reference(h, low_d, W_d, B_d):
    base = mxq(f64(h), 2, "e5m2") @ mxq(f64(W_d), 2, "e5m2").transpose(0, 2, 1)
    delta = f64(low_d) @ f64(B_d).transpose(0, 2, 1)
    out = base + SCALE * delta
    return out.reshape(-1, H)

@@ -1,0 +1,239 @@
+from contextlib import ExitStack
+
+import concourse.masks as masks
+import concourse.mybir as mybir
+
+E, T, H, D, R = 4, 256, 1024, 1024, 128
+FLOPS = 2 * E * T * H * (D + R)
+
+F32 = mybir.dt.float32
+BF16 = mybir.dt.bfloat16
+U32 = mybir.dt.uint32
+U8 = mybir.dt.uint8
+E5M2X4 = mybir.dt.float8_e5m2_x4
+
+P = 128
+K_PASS = 512
+PASSES = D // K_PASS
+N_TILE = 512
+HALVES = H // N_TILE
+TOK_TILES = T // P
+SLOTS = N_TILE // P
+
+FIRST_UNIT_AFTER = 10
+BANKS_PER_UNIT = 3
+VECTOR_BANKS = (0, 3, 8)
+
+
+def bank_list(e):
+    banks = [("h", e, 0, g, 0) for g in range(PASSES)]
+    for j in range(HALVES):
+        banks += [("w", e, j, g, sp) for sp in range(2) for g in range(PASSES)]
+        banks.append(("b", e, j, 0, 0))
+    return banks
+
+
+def schedule():
+    banks = [b for e in range(E) for b in bank_list(e)]
+    units = [(e, j, a) for e in range(E) for j in range(HALVES) for a in range(TOK_TILES)]
+    unit_after = dict((FIRST_UNIT_AFTER - 1 + BANKS_PER_UNIT * n, u) for n, u in enumerate(units))
+    ops = []
+    late = []
+
+    def unit(e, j, a):
+        ops.append(("delta", e, j, a, 0))
+        ops.append(("mx", e, j, a, 0))
+        ops.append(("mx", e, j, a, 1))
+        ops.append(("delta_out", e, j, a, 0))
+
+    for i, bank in enumerate(banks):
+        kind, e, j, g, sp = bank
+        ops.append(("transpose",) + bank)
+        ops.append(("copy",) + bank)
+        now = list(late)
+        late.clear()
+        if kind == "h" and g == PASSES - 1:
+            late.append(("quant_h", e, 0, 0, 0))
+        if kind == "w" and sp == 1:
+            late.append(("quant_w", e, j, g, 0))
+        ops.extend(now)
+        if i in unit_after and i < len(banks) - 1:
+            unit(*unit_after[i])
+            ops.extend(late)
+            late.clear()
+            late.append(("sum",) + unit_after[i] + (0,))
+    ops.extend(late)
+    rest = [u for i, u in sorted(unit_after.items()) if i >= len(banks) - 1]
+    for u in rest[:-TOK_TILES]:
+        unit(*u)
+        ops.append(("sum",) + u + (0,))
+    e, j = E - 1, HALVES - 1
+    for a in range(TOK_TILES):
+        ops.append(("delta", e, j, a, 0))
+    for a in range(TOK_TILES):
+        ops.append(("delta_out", e, j, a, 0))
+    for g in range(PASSES):
+        for a in range(TOK_TILES):
+            ops.append(("mx", e, j, a, g))
+    for a in range(TOK_TILES):
+        ops.append(("sum", e, j, a, 0))
+    return ops
+
+
+def tile_loralinearexpertswrapper_pb_kernel(tc, h, low_d, W_d, B_d, out):
+    nc = tc.nc
+    out_v = out.rearrange("(e p a) n -> e p a n", e=E, a=TOK_TILES)
+
+    with ExitStack() as ctx:
+        ctx.enter_context(tc.manual_schedule())
+        const = ctx.enter_context(tc.tile_pool(name="const", bufs=1))
+        loads = ctx.enter_context(tc.tile_pool(name="loads", bufs=1))
+        work = ctx.enter_context(tc.tile_pool(name="work", bufs=4))
+        results = ctx.enter_context(tc.tile_pool(name="results", bufs=1))
+        tp_pool = ctx.enter_context(tc.psum_pool(name="tp", bufs=4))
+        acc_pool = ctx.enter_context(tc.psum_pool(name="acc", bufs=2))
+        dl_pool = ctx.enter_context(tc.psum_pool(name="dl", bufs=2))
+
+        h_sb, w_sb, b_sb = {}, {}, {}
+        low_sb = loads.tile([P, E, TOK_TILES * R], BF16, name="low_sb")
+        for e in range(E):
+            h_sb[e] = loads.tile([P, TOK_TILES, D], BF16, name="h_sb%d" % e)
+            nc.sync.dma_start(out=h_sb[e][:], in_=h[e].rearrange("(p a) k -> p a k", a=TOK_TILES))
+            for j in range(HALVES):
+                rows = W_d[e, j * N_TILE : (j + 1) * N_TILE, :].rearrange("(p s) k -> p s k", s=SLOTS)
+                for sp in range(2):
+                    w_sb[e, j, sp] = loads.tile([P, 2, D], BF16, name="w_sb%d%d%d" % (e, j, sp))
+                    nc.sync.dma_start(out=w_sb[e, j, sp][:], in_=rows[:, 2 * sp : 2 * sp + 2, :])
+                if j == 0:
+                    if e == 0:
+                        nc.sync.dma_start(
+                            out=low_sb[:], in_=low_d.rearrange("e (p a) r -> p e (a r)", a=TOK_TILES)
+                        )
+                    b_sb[e] = loads.tile([P, HALVES, SLOTS * R], BF16, name="b_sb%d" % e)
+                    nc.sync.dma_start(
+                        out=b_sb[e][:], in_=B_d[e].rearrange("(j p s) r -> p j (s r)", j=HALVES, s=SLOTS)
+                    )
+
+        ident_f32 = const.tile([P, P], F32, name="ident_f32")
+        masks.make_identity(nc, ident_f32[:])
+        ident_bf16 = const.tile([P, P], BF16, name="ident_bf16")
+        masks.make_identity(nc, ident_bf16[:])
+
+        warm = const.tile([P, 8], F32, name="warm")
+        nc.vector.memset(warm[:], 0.0)
+        warm_out = const.tile([P, 8], F32, name="warm_out")
+        nc.scalar.activation(out=warm_out[:], in_=warm[:], func=mybir.ActivationFunctionType.Copy, scale=2.0)
+
+        tp, grouped, codes, scales, plain_t, acc, dl, dl_sb = {}, {}, {}, {}, {}, {}, {}, {}
+
+        def transpose_words(dst, src, g):
+            for x in range(2):
+                words = src[:, x, :].bitcast(F32)
+                for u in range(2):
+                    nc.tensor.transpose(
+                        dst[:, x, u, :], words[:, 256 * g + u : 256 * (g + 1) : 2], ident_f32[:]
+                    )
+
+        for step in schedule():
+            op = step[0]
+            if op == "transpose":
+                kind, e, j, g, sp = step[1:]
+                if kind == "b":
+                    n = SLOTS + (TOK_TILES if j == 0 else 0)
+                    t = tp_pool.tile([P, n, P], BF16, name="tp_b", tag="tp")
+                    if j == 0:
+                        for a in range(TOK_TILES):
+                            nc.tensor.transpose(t[:, a, :], low_sb[:, e, a * R : (a + 1) * R], ident_bf16[:])
+                    for s in range(SLOTS):
+                        nc.tensor.transpose(
+                            t[:, n - SLOTS + s, :], b_sb[e][:, j, s * R : (s + 1) * R], ident_bf16[:]
+                        )
+                else:
+                    t = tp_pool.tile([P, 2, 2, P], F32, name="tp_w", tag="tp")
+                    transpose_words(t, h_sb[e] if kind == "h" else w_sb[e, j, sp], g)
+                tp[step[1:]] = t
+            elif op == "copy":
+                kind, e, j, g, sp = step[1:]
+                t = tp[step[1:]]
+                if kind == "b":
+                    n = SLOTS + (TOK_TILES if j == 0 else 0)
+                    plain_t[e, j] = work.tile([P, n * P], BF16, name="plain_t%d" % j, bufs=2)
+                    nc.scalar.copy(out=plain_t[e, j][:], in_=t[:].rearrange("p n r -> p (n r)"))
+                else:
+                    if kind == "h":
+                        if g == 0:
+                            grouped["h", e, 0] = work.tile([P, PASSES, T, 2], F32, name="grouped_h", bufs=2, align_bytes=64)
+                        dst = grouped["h", e, 0][:, g, :, :]
+                    else:
+                        if g == 0 and sp == 0:
+                            grouped["w", e, j] = work.tile(
+                                [P, PASSES, N_TILE, 2], F32, name="grouped_w", align_bytes=64
+                            )
+                        dst = grouped["w", e, j][:, g, 2 * P * sp : 2 * P * (sp + 1), :]
+                    dst = dst.rearrange("p (x r) u -> p x r u", x=2)
+                    src = t[:].rearrange("p x u r -> p x r u")
+                    if bank_list(e).index(step[1:]) in VECTOR_BANKS:
+                        nc.vector.tensor_copy(out=dst, in_=src)
+                    else:
+                        nc.scalar.copy(out=dst, in_=src)
+            elif op == "quant_h":
+                e = step[1]
+                codes["h", e, 0] = work.tile([P, PASSES, T], U32, name="codes_h", bufs=2, align_bytes=64)
+                scales["h", e, 0] = work.tile([P, PASSES, T], U8, name="scales_h", bufs=2, align_bytes=64)
+                nc.vector.quantize_mx(
+                    out=codes["h", e, 0][:].rearrange("p g c -> p (g c)").bitcast(E5M2X4),
+                    scales=scales["h", e, 0][:].rearrange("p g c -> p (g c)"),
+                    in_=grouped["h", e, 0][:].rearrange("p g c u -> p (g c u)").bitcast(BF16),
+                )
+            elif op == "quant_w":
+                e, j, g = step[1:4]
+                if g == 0:
+                    codes["w", e, j] = work.tile([P, PASSES, N_TILE], U32, name="codes_w", align_bytes=64)
+                    scales["w", e, j] = work.tile([P, PASSES, N_TILE], U8, name="scales_w", align_bytes=64)
+                nc.vector.quantize_mx(
+                    out=codes["w", e, j][:, g, :].bitcast(E5M2X4),
+                    scales=scales["w", e, j][:, g, :],
+                    in_=grouped["w", e, j][:, g, :, :].rearrange("p c u -> p (c u)").bitcast(BF16),
+                )
+            elif op == "delta":
+                e, j, a = step[1:4]
+                dl[e, j, a] = dl_pool.tile([P, N_TILE], F32, name="dl")
+                nc.tensor.matmul(
+                    dl[e, j, a][:],
+                    lhsT=plain_t[e, 0][:, a * P : (a + 1) * P],
+                    rhs=plain_t[e, 0][:, TOK_TILES * P :] if j == 0 else plain_t[e, 1][:],
+                    start=True,
+                    stop=True,
+                )
+            elif op == "delta_out":
+                e, j, a = step[1:4]
+                dl_sb[e, j, a] = work.tile([P, N_TILE], F32, name="dl_sb")
+                nc.scalar.activation(
+                    out=dl_sb[e, j, a][:].rearrange("p (r s) -> p r s", s=SLOTS),
+                    in_=dl[e, j, a][:].rearrange("p (s r) -> p r s", s=SLOTS),
+                    func=mybir.ActivationFunctionType.Copy,
+                    scale=2.0,
+                )
+            elif op == "mx":
+                e, j, a, g = step[1:]
+                if g == 0:
+                    acc[e, j, a] = acc_pool.tile([P, N_TILE], F32, name="acc")
+                nc.tensor.matmul_mx(
+                    out=acc[e, j, a][:],
+                    lhsT=codes["h", e, 0][:, g, a * P : (a + 1) * P].bitcast(E5M2X4),
+                    lhsT_scale=scales["h", e, 0][:, g, a * P : (a + 1) * P],
+                    rhs=codes["w", e, j][:, g, :].bitcast(E5M2X4),
+                    rhs_scale=scales["w", e, j][:, g, :],
+                    start=(g == 0),
+                    stop=(g == PASSES - 1),
+                )
+            elif op == "sum":
+                e, j, a = step[1:4]
+                res = results.tile([P, N_TILE], F32, name="res%d%d%d" % (e, j, a))
+                nc.vector.tensor_tensor(
+                    out=res[:].rearrange("p (r s) -> p r s", s=SLOTS),
+                    in0=acc[e, j, a][:].rearrange("p (s r) -> p r s", s=SLOTS),
+                    in1=dl_sb[e, j, a][:].rearrange("p (r s) -> p r s", s=SLOTS),
+                    op=mybir.AluOpType.add,
+                )
+                nc.sync.dma_start(out=out_v[e][:, a, j * N_TILE : (j + 1) * N_TILE], in_=res[:])

@@ -20,9 +20,10 @@ HALVES = H // N_TILE
 TOK_TILES = T // P
 SLOTS = N_TILE // P
 
-FIRST_UNIT_AFTER = 10
+FIRST_UNIT_AFTER = 12
 BANKS_PER_UNIT = 3
-VECTOR_BANKS = (0, 3, 8)
+PERMUTE_AHEAD = 4
+VECTOR_BANKS = (1, 3, 5, 8, 10)
 
 
 def bank_list(e):
@@ -31,6 +32,15 @@ def bank_list(e):
         banks += [("w", e, j, g, sp) for sp in range(2) for g in range(PASSES)]
         banks.append(("b", e, j, 0, 0))
     return banks
+
+
+def load_of(bank):
+    kind, e, j, g, sp = bank
+    return (kind, e, j, 0, sp)
+
+
+def is_permuted(bank):
+    return bank[0] != "b" and bank[1] > 0
 
 
 def schedule():
@@ -46,10 +56,19 @@ def schedule():
         ops.append(("mx", e, j, a, 1))
         ops.append(("delta_out", e, j, a, 0))
 
+    def permute(bank):
+        step = ("permute",) + load_of(bank)
+        if is_permuted(bank) and step not in ops:
+            ops.append(step)
+
+    for bank in banks[:PERMUTE_AHEAD]:
+        permute(bank)
     for i, bank in enumerate(banks):
         kind, e, j, g, sp = bank
         ops.append(("transpose",) + bank)
         ops.append(("copy",) + bank)
+        for ahead in banks[i + PERMUTE_AHEAD : i + PERMUTE_AHEAD + 1]:
+            permute(ahead)
         now = list(late)
         late.clear()
         if kind == "h" and g == PASSES - 1:
@@ -88,14 +107,13 @@ def tile_loralinearexpertswrapper_pb_kernel(tc, h, low_d, W_d, B_d, out):
         ctx.enter_context(tc.manual_schedule())
         const = ctx.enter_context(tc.tile_pool(name="const", bufs=1))
         loads = ctx.enter_context(tc.tile_pool(name="loads", bufs=1))
-        work = ctx.enter_context(tc.tile_pool(name="work", bufs=4))
-        results = ctx.enter_context(tc.tile_pool(name="results", bufs=1))
+        work = ctx.enter_context(tc.tile_pool(name="work", bufs=3))
+        results = ctx.enter_context(tc.tile_pool(name="results", bufs=8))
         tp_pool = ctx.enter_context(tc.psum_pool(name="tp", bufs=4))
         acc_pool = ctx.enter_context(tc.psum_pool(name="acc", bufs=2))
         dl_pool = ctx.enter_context(tc.psum_pool(name="dl", bufs=2))
 
-        h_sb, w_sb, b_sb = {}, {}, {}
-        low_sb = loads.tile([P, E, TOK_TILES * R], BF16, name="low_sb")
+        h_sb, w_sb, b_sb, low_sb = {}, {}, {}, {}
         for e in range(E):
             h_sb[e] = loads.tile([P, TOK_TILES, D], BF16, name="h_sb%d" % e)
             nc.sync.dma_start(out=h_sb[e][:], in_=h[e].rearrange("(p a) k -> p a k", a=TOK_TILES))
@@ -105,10 +123,8 @@ def tile_loralinearexpertswrapper_pb_kernel(tc, h, low_d, W_d, B_d, out):
                     w_sb[e, j, sp] = loads.tile([P, 2, D], BF16, name="w_sb%d%d%d" % (e, j, sp))
                     nc.sync.dma_start(out=w_sb[e, j, sp][:], in_=rows[:, 2 * sp : 2 * sp + 2, :])
                 if j == 0:
-                    if e == 0:
-                        nc.sync.dma_start(
-                            out=low_sb[:], in_=low_d.rearrange("e (p a) r -> p e (a r)", a=TOK_TILES)
-                        )
+                    low_sb[e] = loads.tile([P, TOK_TILES * R], BF16, name="low_sb%d" % e)
+                    nc.sync.dma_start(out=low_sb[e][:], in_=low_d[e].rearrange("(p a) r -> p (a r)", a=TOK_TILES))
                     b_sb[e] = loads.tile([P, HALVES, SLOTS * R], BF16, name="b_sb%d" % e)
                     nc.sync.dma_start(
                         out=b_sb[e][:], in_=B_d[e].rearrange("(j p s) r -> p j (s r)", j=HALVES, s=SLOTS)
@@ -124,33 +140,47 @@ def tile_loralinearexpertswrapper_pb_kernel(tc, h, low_d, W_d, B_d, out):
         warm_out = const.tile([P, 8], F32, name="warm_out")
         nc.scalar.activation(out=warm_out[:], in_=warm[:], func=mybir.ActivationFunctionType.Copy, scale=2.0)
 
-        tp, grouped, codes, scales, plain_t, acc, dl, dl_sb = {}, {}, {}, {}, {}, {}, {}, {}
+        tp, ordered, grouped, codes, scales, plain_t, acc, dl, dl_sb = {}, {}, {}, {}, {}, {}, {}, {}, {}
 
-        def transpose_words(dst, src, g):
+        def transpose_words(dst, bank):
+            kind, e, j, g, sp = bank
             for x in range(2):
-                words = src[:, x, :].bitcast(F32)
                 for u in range(2):
-                    nc.tensor.transpose(
-                        dst[:, x, u, :], words[:, 256 * g + u : 256 * (g + 1) : 2], ident_f32[:]
-                    )
+                    if is_permuted(bank):
+                        words = ordered[load_of(bank)][:, PASSES * x + g, u, :]
+                    else:
+                        src = h_sb[e] if kind == "h" else w_sb[e, j, sp]
+                        words = src[:, x, :].bitcast(F32)[:, 256 * g + u : 256 * (g + 1) : 2]
+                    nc.tensor.transpose(dst[:, x, u, :], words, ident_f32[:])
 
         for step in schedule():
             op = step[0]
-            if op == "transpose":
+            if op == "permute":
+                kind, e, j, g, sp = step[1:]
+                src = h_sb[e] if kind == "h" else w_sb[e, j, sp]
+                ordered[step[1:]] = work.tile([P, 2 * PASSES, 2, P], F32, name="ordered", bufs=5)
+                nc.vector.tensor_copy(
+                    out=ordered[step[1:]][:],
+                    in_=src[:]
+                    .rearrange("p x k -> p (x k)")
+                    .bitcast(F32)
+                    .rearrange("p (y q u) -> p y u q", y=2 * PASSES, u=2),
+                )
+            elif op == "transpose":
                 kind, e, j, g, sp = step[1:]
                 if kind == "b":
                     n = SLOTS + (TOK_TILES if j == 0 else 0)
                     t = tp_pool.tile([P, n, P], BF16, name="tp_b", tag="tp")
                     if j == 0:
                         for a in range(TOK_TILES):
-                            nc.tensor.transpose(t[:, a, :], low_sb[:, e, a * R : (a + 1) * R], ident_bf16[:])
+                            nc.tensor.transpose(t[:, a, :], low_sb[e][:, a * R : (a + 1) * R], ident_bf16[:])
                     for s in range(SLOTS):
                         nc.tensor.transpose(
                             t[:, n - SLOTS + s, :], b_sb[e][:, j, s * R : (s + 1) * R], ident_bf16[:]
                         )
                 else:
                     t = tp_pool.tile([P, 2, 2, P], F32, name="tp_w", tag="tp")
-                    transpose_words(t, h_sb[e] if kind == "h" else w_sb[e, j, sp], g)
+                    transpose_words(t, step[1:])
                 tp[step[1:]] = t
             elif op == "copy":
                 kind, e, j, g, sp = step[1:]
@@ -172,7 +202,7 @@ def tile_loralinearexpertswrapper_pb_kernel(tc, h, low_d, W_d, B_d, out):
                         dst = grouped["w", e, j][:, g, 2 * P * sp : 2 * P * (sp + 1), :]
                     dst = dst.rearrange("p (x r) u -> p x r u", x=2)
                     src = t[:].rearrange("p x u r -> p x r u")
-                    if bank_list(e).index(step[1:]) in VECTOR_BANKS:
+                    if e == 0 and bank_list(e).index(step[1:]) in VECTOR_BANKS:
                         nc.vector.tensor_copy(out=dst, in_=src)
                     else:
                         nc.scalar.copy(out=dst, in_=src)
@@ -229,7 +259,7 @@ def tile_loralinearexpertswrapper_pb_kernel(tc, h, low_d, W_d, B_d, out):
                 )
             elif op == "sum":
                 e, j, a = step[1:4]
-                res = results.tile([P, N_TILE], F32, name="res%d%d%d" % (e, j, a))
+                res = results.tile([P, N_TILE], F32, name="res")
                 nc.vector.tensor_tensor(
                     out=res[:].rearrange("p (r s) -> p r s", s=SLOTS),
                     in0=acc[e, j, a][:].rearrange("p (s r) -> p r s", s=SLOTS),

@@ -20,10 +20,11 @@ HALVES = H // N_TILE
 TOK_TILES = T // P
 SLOTS = N_TILE // P
 
-FIRST_UNIT_AFTER = 12
-BANKS_PER_UNIT = 3
+FIRST_GROUP_AFTER = 12
+BANKS_PER_GROUP = 6
 PERMUTE_AHEAD = 4
-VECTOR_BANKS = (1, 3, 5, 8, 10)
+VECTOR_BANKS_FIRST = (1, 3, 5, 8, 10)
+VECTOR_BANKS = (3, 8)
 
 
 def bank_list(e):
@@ -40,52 +41,66 @@ def load_of(bank):
 
 
 def is_permuted(bank):
-    return bank[0] != "b" and bank[1] > 0
+    kind, e, j, g, sp = bank
+    return kind == "w" and e > 0 and sp == 0
+
+
+def on_vector(bank):
+    e = bank[1]
+    return bank[0] != "b" and bank_list(e).index(bank) in (VECTOR_BANKS if e > 0 else VECTOR_BANKS_FIRST)
 
 
 def schedule():
     banks = [b for e in range(E) for b in bank_list(e)]
-    units = [(e, j, a) for e in range(E) for j in range(HALVES) for a in range(TOK_TILES)]
-    unit_after = dict((FIRST_UNIT_AFTER - 1 + BANKS_PER_UNIT * n, u) for n, u in enumerate(units))
+    halves = [(e, j) for e in range(E) for j in range(HALVES)]
+    group_after = dict((FIRST_GROUP_AFTER - 1 + BANKS_PER_GROUP * n, r) for n, r in enumerate(halves))
     ops = []
     late = []
 
-    def unit(e, j, a):
-        ops.append(("delta", e, j, a, 0))
-        ops.append(("mx", e, j, a, 0))
-        ops.append(("mx", e, j, a, 1))
-        ops.append(("delta_out", e, j, a, 0))
+    def flush(now):
+        due = [x for x in late if x[0] <= now]
+        for x in due:
+            late.remove(x)
+            ops.append(x[1])
 
     def permute(bank):
         step = ("permute",) + load_of(bank)
         if is_permuted(bank) and step not in ops:
             ops.append(step)
 
+    def group(e, j, now):
+        ops.append(("delta", e, j, 0, 0))
+        for a in range(TOK_TILES):
+            for g in range(PASSES):
+                ops.append(("mx", e, j, a, g))
+        ops.append(("delta", e, j, 1, 0))
+        for a in range(TOK_TILES):
+            ops.append(("delta_out", e, j, a, 0))
+            late.append((now + 1 + a, ("sum", e, j, a, 0)))
+
     for bank in banks[:PERMUTE_AHEAD]:
         permute(bank)
+    now = 0
     for i, bank in enumerate(banks):
         kind, e, j, g, sp = bank
         ops.append(("transpose",) + bank)
         ops.append(("copy",) + bank)
         for ahead in banks[i + PERMUTE_AHEAD : i + PERMUTE_AHEAD + 1]:
             permute(ahead)
-        now = list(late)
-        late.clear()
         if kind == "h" and g == PASSES - 1:
-            late.append(("quant_h", e, 0, 0, 0))
+            late.append((now + 1, ("quant_h", e, 0, 0, 0)))
         if kind == "w" and sp == 1:
-            late.append(("quant_w", e, j, g, 0))
-        ops.extend(now)
-        if i in unit_after and i < len(banks) - 1:
-            unit(*unit_after[i])
-            ops.extend(late)
-            late.clear()
-            late.append(("sum",) + unit_after[i] + (0,))
-    ops.extend(late)
-    rest = [u for i, u in sorted(unit_after.items()) if i >= len(banks) - 1]
-    for u in rest[:-TOK_TILES]:
-        unit(*u)
-        ops.append(("sum",) + u + (0,))
+            late.append((now + 1, ("quant_w", e, j, g, 0)))
+        flush(now)
+        now += 1
+        if i in group_after and i < len(banks) - 1:
+            group(group_after[i][0], group_after[i][1], now)
+            flush(now)
+            now += 1
+    flush(now + TOK_TILES)
+    for e, j in [r for i, r in sorted(group_after.items()) if i >= len(banks) - 1][:-1]:
+        group(e, j, now)
+        flush(now + TOK_TILES)
     e, j = E - 1, HALVES - 1
     for a in range(TOK_TILES):
         ops.append(("delta", e, j, a, 0))
@@ -202,7 +217,7 @@ def tile_loralinearexpertswrapper_pb_kernel(tc, h, low_d, W_d, B_d, out):
                         dst = grouped["w", e, j][:, g, 2 * P * sp : 2 * P * (sp + 1), :]
                     dst = dst.rearrange("p (x r) u -> p x r u", x=2)
                     src = t[:].rearrange("p x u r -> p x r u")
-                    if e == 0 and bank_list(e).index(step[1:]) in VECTOR_BANKS:
+                    if on_vector(step[1:]):
                         nc.vector.tensor_copy(out=dst, in_=src)
                     else:
                         nc.scalar.copy(out=dst, in_=src)

@@ -20,11 +20,11 @@ HALVES = H // N_TILE
 TOK_TILES = T // P
 SLOTS = N_TILE // P
 
-FIRST_GROUP_AFTER = 12
-BANKS_PER_GROUP = 6
+FIRST_UNIT_AFTER = 12
+BANKS_PER_UNIT = 3
 PERMUTE_AHEAD = 4
 VECTOR_BANKS_FIRST = (1, 3, 5, 8, 10)
-VECTOR_BANKS = (3, 8)
+VECTOR_BANKS = (8,)
 
 
 def bank_list(e):
@@ -42,7 +42,7 @@ def load_of(bank):
 
 def is_permuted(bank):
     kind, e, j, g, sp = bank
-    return kind == "w" and e > 0 and sp == 0
+    return kind == "w" and e > 0 and (j, sp) != (1, 0)
 
 
 def on_vector(bank):
@@ -52,55 +52,47 @@ def on_vector(bank):
 
 def schedule():
     banks = [b for e in range(E) for b in bank_list(e)]
-    halves = [(e, j) for e in range(E) for j in range(HALVES)]
-    group_after = dict((FIRST_GROUP_AFTER - 1 + BANKS_PER_GROUP * n, r) for n, r in enumerate(halves))
+    units = [(e, j, a) for e in range(E) for j in range(HALVES) for a in range(TOK_TILES)]
+    unit_after = dict((FIRST_UNIT_AFTER - 1 + BANKS_PER_UNIT * n, u) for n, u in enumerate(units))
     ops = []
     late = []
 
-    def flush(now):
-        due = [x for x in late if x[0] <= now]
-        for x in due:
-            late.remove(x)
-            ops.append(x[1])
+    def unit(e, j, a):
+        ops.append(("delta", e, j, a, 0))
+        ops.append(("mx", e, j, a, 0))
+        ops.append(("mx", e, j, a, 1))
+        ops.append(("delta_out", e, j, a, 0))
 
     def permute(bank):
         step = ("permute",) + load_of(bank)
         if is_permuted(bank) and step not in ops:
             ops.append(step)
 
-    def group(e, j, now):
-        ops.append(("delta", e, j, 0, 0))
-        for a in range(TOK_TILES):
-            for g in range(PASSES):
-                ops.append(("mx", e, j, a, g))
-        ops.append(("delta", e, j, 1, 0))
-        for a in range(TOK_TILES):
-            ops.append(("delta_out", e, j, a, 0))
-            late.append((now + 1 + a, ("sum", e, j, a, 0)))
-
     for bank in banks[:PERMUTE_AHEAD]:
         permute(bank)
-    now = 0
     for i, bank in enumerate(banks):
         kind, e, j, g, sp = bank
         ops.append(("transpose",) + bank)
         ops.append(("copy",) + bank)
         for ahead in banks[i + PERMUTE_AHEAD : i + PERMUTE_AHEAD + 1]:
             permute(ahead)
+        now = list(late)
+        late.clear()
         if kind == "h" and g == PASSES - 1:
-            late.append((now + 1, ("quant_h", e, 0, 0, 0)))
+            late.append(("quant_h", e, 0, 0, 0))
         if kind == "w" and sp == 1:
-            late.append((now + 1, ("quant_w", e, j, g, 0)))
-        flush(now)
-        now += 1
-        if i in group_after and i < len(banks) - 1:
-            group(group_after[i][0], group_after[i][1], now)
-            flush(now)
-            now += 1
-    flush(now + TOK_TILES)
-    for e, j in [r for i, r in sorted(group_after.items()) if i >= len(banks) - 1][:-1]:
-        group(e, j, now)
-        flush(now + TOK_TILES)
+            late.append(("quant_w", e, j, g, 0))
+        ops.extend(now)
+        if i in unit_after and i < len(banks) - 1:
+            unit(*unit_after[i])
+            ops.extend(late)
+            late.clear()
+            late.append(("sum",) + unit_after[i] + (0,))
+    ops.extend(late)
+    rest = [u for i, u in sorted(unit_after.items()) if i >= len(banks) - 1]
+    for u in rest[:-TOK_TILES]:
+        unit(*u)
+        ops.append(("sum",) + u + (0,))
     e, j = E - 1, HALVES - 1
     for a in range(TOK_TILES):
         ops.append(("delta", e, j, a, 0))

@@ -20,6 +20,7 @@ HALVES = H // N_TILE
 TOK_TILES = T // P
 SLOTS = N_TILE // P
 
+LAST_PIECES = 2
 FIRST_UNIT_AFTER = 12
 BANKS_PER_UNIT = 3
 PERMUTE_AHEAD = 4
@@ -50,10 +51,22 @@ def on_vector(bank):
     return bank[0] != "b" and bank_list(e).index(bank) in (VECTOR_BANKS if e > 0 else VECTOR_BANKS_FIRST)
 
 
-def schedule():
-    banks = [b for e in range(E) for b in bank_list(e)]
+def all_banks():
+    return [b for e in range(E) for b in bank_list(e)]
+
+
+def units_by_bank():
     units = [(e, j, a) for e in range(E) for j in range(HALVES) for a in range(TOK_TILES)]
-    unit_after = dict((FIRST_UNIT_AFTER - 1 + BANKS_PER_UNIT * n, u) for n, u in enumerate(units))
+    return dict((FIRST_UNIT_AFTER - 1 + BANKS_PER_UNIT * n, u) for n, u in enumerate(units))
+
+
+def units_after_all_banks():
+    return [u for i, u in sorted(units_by_bank().items()) if i >= len(all_banks()) - 1]
+
+
+def schedule():
+    banks = all_banks()
+    unit_after = units_by_bank()
     ops = []
     late = []
 
@@ -89,20 +102,9 @@ def schedule():
             late.clear()
             late.append(("sum",) + unit_after[i] + (0,))
     ops.extend(late)
-    rest = [u for i, u in sorted(unit_after.items()) if i >= len(banks) - 1]
-    for u in rest[:-TOK_TILES]:
+    for u in units_after_all_banks():
         unit(*u)
         ops.append(("sum",) + u + (0,))
-    e, j = E - 1, HALVES - 1
-    for a in range(TOK_TILES):
-        ops.append(("delta", e, j, a, 0))
-    for a in range(TOK_TILES):
-        ops.append(("delta_out", e, j, a, 0))
-    for g in range(PASSES):
-        for a in range(TOK_TILES):
-            ops.append(("mx", e, j, a, g))
-    for a in range(TOK_TILES):
-        ops.append(("sum", e, j, a, 0))
     return ops
 
 
@@ -254,7 +256,10 @@ def tile_loralinearexpertswrapper_pb_kernel(tc, h, low_d, W_d, B_d, out):
             elif op == "mx":
                 e, j, a, g = step[1:]
                 if g == 0:
-                    acc[e, j, a] = acc_pool.tile([P, N_TILE], F32, name="acc")
+                    if (e, j, a) in units_after_all_banks():
+                        acc[e, j, a] = tp_pool.tile([P, N_TILE], F32, name="acc_late", tag="tp")
+                    else:
+                        acc[e, j, a] = acc_pool.tile([P, N_TILE], F32, name="acc")
                 nc.tensor.matmul_mx(
                     out=acc[e, j, a][:],
                     lhsT=codes["h", e, 0][:, g, a * P : (a + 1) * P].bitcast(E5M2X4),
@@ -267,10 +272,16 @@ def tile_loralinearexpertswrapper_pb_kernel(tc, h, low_d, W_d, B_d, out):
             elif op == "sum":
                 e, j, a = step[1:4]
                 res = results.tile([P, N_TILE], F32, name="res")
-                nc.vector.tensor_tensor(
-                    out=res[:].rearrange("p (r s) -> p r s", s=SLOTS),
-                    in0=acc[e, j, a][:].rearrange("p (s r) -> p r s", s=SLOTS),
-                    in1=dl_sb[e, j, a][:].rearrange("p (r s) -> p r s", s=SLOTS),
-                    op=mybir.AluOpType.add,
-                )
-                nc.sync.dma_start(out=out_v[e][:, a, j * N_TILE : (j + 1) * N_TILE], in_=res[:])
+                pieces = LAST_PIECES if (e, j, a) == (E - 1, HALVES - 1, TOK_TILES - 1) else 1
+                rows = P // pieces
+                for c in range(pieces):
+                    nc.vector.tensor_tensor(
+                        out=res[:, c * rows * SLOTS : (c + 1) * rows * SLOTS].rearrange("p (r s) -> p r s", s=SLOTS),
+                        in0=acc[e, j, a][:].rearrange("p (s r) -> p r s", s=SLOTS)[:, c * rows : (c + 1) * rows, :],
+                        in1=dl_sb[e, j, a][:, c * rows * SLOTS : (c + 1) * rows * SLOTS].rearrange("p (r s) -> p r s", s=SLOTS),
+                        op=mybir.AluOpType.add,
+                    )
+                    nc.sync.dma_start(
+                        out=out_v[e][:, a, j * N_TILE + c * rows * SLOTS : j * N_TILE + (c + 1) * rows * SLOTS],
+                        in_=res[:, c * rows * SLOTS : (c + 1) * rows * SLOTS],
+                    )

@@ -20,6 +20,7 @@ HALVES = H // N_TILE
 TOK_TILES = T // P
 SLOTS = N_TILE // P
 
+WHOLE_HALVES_FROM = 2
 LAST_PIECES = 2
 FIRST_UNIT_AFTER = 12
 BANKS_PER_UNIT = 3
@@ -117,20 +118,28 @@ def tile_loralinearexpertswrapper_pb_kernel(tc, h, low_d, W_d, B_d, out):
         const = ctx.enter_context(tc.tile_pool(name="const", bufs=1))
         loads = ctx.enter_context(tc.tile_pool(name="loads", bufs=1))
         work = ctx.enter_context(tc.tile_pool(name="work", bufs=3))
-        results = ctx.enter_context(tc.tile_pool(name="results", bufs=8))
+        results = ctx.enter_context(tc.tile_pool(name="results", bufs=4))
         tp_pool = ctx.enter_context(tc.psum_pool(name="tp", bufs=4))
         acc_pool = ctx.enter_context(tc.psum_pool(name="acc", bufs=2))
         dl_pool = ctx.enter_context(tc.psum_pool(name="dl", bufs=2))
 
         h_sb, w_sb, b_sb, low_sb = {}, {}, {}, {}
         for e in range(E):
-            h_sb[e] = loads.tile([P, TOK_TILES, D], BF16, name="h_sb%d" % e)
-            nc.sync.dma_start(out=h_sb[e][:], in_=h[e].rearrange("(p a) k -> p a k", a=TOK_TILES))
+            h_pair = loads.tile([P, TOK_TILES, D], BF16, name="h_pair%d" % e)
+            nc.sync.dma_start(out=h_pair[:], in_=h[e].rearrange("(p a) k -> p a k", a=TOK_TILES))
+            h_sb[e] = h_pair[:]
             for j in range(HALVES):
                 rows = W_d[e, j * N_TILE : (j + 1) * N_TILE, :].rearrange("(p s) k -> p s k", s=SLOTS)
-                for sp in range(2):
-                    w_sb[e, j, sp] = loads.tile([P, 2, D], BF16, name="w_sb%d%d%d" % (e, j, sp))
-                    nc.sync.dma_start(out=w_sb[e, j, sp][:], in_=rows[:, 2 * sp : 2 * sp + 2, :])
+                if e >= WHOLE_HALVES_FROM:
+                    w_half = loads.tile([P, SLOTS, D], BF16, name="w_half%d%d" % (e, j))
+                    nc.sync.dma_start(out=w_half[:], in_=rows)
+                    for sp in range(2):
+                        w_sb[e, j, sp] = w_half[:, 2 * sp : 2 * sp + 2, :]
+                else:
+                    for sp in range(2):
+                        w_pair = loads.tile([P, 2, D], BF16, name="w_pair%d%d%d" % (e, j, sp))
+                        nc.sync.dma_start(out=w_pair[:], in_=rows[:, 2 * sp : 2 * sp + 2, :])
+                        w_sb[e, j, sp] = w_pair[:]
                 if j == 0:
                     low_sb[e] = loads.tile([P, TOK_TILES * R], BF16, name="low_sb%d" % e)
                     nc.sync.dma_start(out=low_sb[e][:], in_=low_d[e].rearrange("(p a) r -> p (a r)", a=TOK_TILES))
@@ -149,7 +158,7 @@ def tile_loralinearexpertswrapper_pb_kernel(tc, h, low_d, W_d, B_d, out):
         warm_out = const.tile([P, 8], F32, name="warm_out")
         nc.scalar.activation(out=warm_out[:], in_=warm[:], func=mybir.ActivationFunctionType.Copy, scale=2.0)
 
-        tp, ordered, grouped, codes, scales, plain_t, acc, dl, dl_sb = {}, {}, {}, {}, {}, {}, {}, {}, {}
+        tp, ordered, grouped, codes, scales, plain_t, acc, dl, dl_sb, res_all = {}, {}, {}, {}, {}, {}, {}, {}, {}, {}
 
         def transpose_words(dst, bank):
             kind, e, j, g, sp = bank
@@ -170,8 +179,7 @@ def tile_loralinearexpertswrapper_pb_kernel(tc, h, low_d, W_d, B_d, out):
                 ordered[step[1:]] = work.tile([P, 2 * PASSES, 2, P], F32, name="ordered", bufs=5)
                 nc.vector.tensor_copy(
                     out=ordered[step[1:]][:],
-                    in_=src[:]
-                    .rearrange("p x k -> p (x k)")
+                    in_=src.rearrange("p x k -> p (x k)")
                     .bitcast(F32)
                     .rearrange("p (y q u) -> p y u q", y=2 * PASSES, u=2),
                 )
@@ -271,6 +279,18 @@ def tile_loralinearexpertswrapper_pb_kernel(tc, h, low_d, W_d, B_d, out):
                 )
             elif op == "sum":
                 e, j, a = step[1:4]
+                if e < E - 1:
+                    if (j, a) == (0, 0):
+                        res_all[e] = results.tile([P, TOK_TILES, H], F32, name="res_all", bufs=E - 1)
+                    nc.vector.tensor_tensor(
+                        out=res_all[e][:, a, j * N_TILE : (j + 1) * N_TILE].rearrange("p (r s) -> p r s", s=SLOTS),
+                        in0=acc[e, j, a][:].rearrange("p (s r) -> p r s", s=SLOTS),
+                        in1=dl_sb[e, j, a][:].rearrange("p (r s) -> p r s", s=SLOTS),
+                        op=mybir.AluOpType.add,
+                    )
+                    if (j, a) == (HALVES - 1, TOK_TILES - 1):
+                        nc.sync.dma_start(out=out_v[e], in_=res_all[e][:])
+                    continue
                 res = results.tile([P, N_TILE], F32, name="res")
                 pieces = LAST_PIECES if (e, j, a) == (E - 1, HALVES - 1, TOK_TILES - 1) else 1
                 rows = P // pieces

@@ -22,10 +22,11 @@ SLOTS = N_TILE // P
 
 WHOLE_HALVES_FROM = 2
 LAST_PIECES = 2
-FIRST_UNIT_AFTER = 12
-BANKS_PER_UNIT = 3
+FIRST_GROUP_AFTER = 12
+BANKS_PER_RUN = 3
+MATMULS_PER_GROUP = 3
 PERMUTE_AHEAD = 4
-VECTOR_BANKS_FIRST = (1, 3, 5, 8, 10)
+VECTOR_BANKS_FIRST = (1, 3, 5, 8)
 VECTOR_BANKS = (8,)
 
 
@@ -34,6 +35,8 @@ def bank_list(e):
     for j in range(HALVES):
         banks += [("w", e, j, g, sp) for sp in range(2) for g in range(PASSES)]
         banks.append(("b", e, j, 0, 0))
+    if e == 0:
+        banks = [b for b in banks if b[0] != "b"] + [b for b in banks if b[0] == "b"]
     return banks
 
 
@@ -56,26 +59,41 @@ def all_banks():
     return [b for e in range(E) for b in bank_list(e)]
 
 
-def units_by_bank():
-    units = [(e, j, a) for e in range(E) for j in range(HALVES) for a in range(TOK_TILES)]
-    return dict((FIRST_UNIT_AFTER - 1 + BANKS_PER_UNIT * n, u) for n, u in enumerate(units))
+def matmuls_of_tile(e, j, a):
+    steps = [("delta", e, j, a, 0), ("mx", e, j, a, 0), ("mx", e, j, a, 1)]
+    return steps[1:] + steps[:1] if (e, j, a) == (0, 0, 0) else steps
 
 
-def units_after_all_banks():
-    return [u for i, u in sorted(units_by_bank().items()) if i >= len(all_banks()) - 1]
+def all_matmuls():
+    return [
+        step
+        for e in range(E)
+        for j in range(HALVES)
+        for a in range(TOK_TILES)
+        for step in matmuls_of_tile(e, j, a)
+    ]
+
+
+def matmuls_among_banks():
+    runs = -(-(len(all_banks()) - FIRST_GROUP_AFTER) // BANKS_PER_RUN)
+    return runs * MATMULS_PER_GROUP
+
+
+def tiles_after_all_banks():
+    return [m[1:4] for m in all_matmuls()[matmuls_among_banks() :] if m[0] == "mx" and m[4] == 0]
 
 
 def schedule():
     banks = all_banks()
-    unit_after = units_by_bank()
+    matmuls = all_matmuls()
     ops = []
     late = []
+    done = []
 
-    def unit(e, j, a):
-        ops.append(("delta", e, j, a, 0))
-        ops.append(("mx", e, j, a, 0))
-        ops.append(("mx", e, j, a, 1))
-        ops.append(("delta_out", e, j, a, 0))
+    def matmul(m):
+        ops.append(m)
+        if m[0] == "delta":
+            ops.append(("delta_out",) + m[1:])
 
     def permute(bank):
         step = ("permute",) + load_of(bank)
@@ -86,26 +104,31 @@ def schedule():
         permute(bank)
     for i, bank in enumerate(banks):
         kind, e, j, g, sp = bank
+        ahead = i - FIRST_GROUP_AFTER
+        if ahead >= 0 and ahead % BANKS_PER_RUN == 0:
+            first = ahead // BANKS_PER_RUN * MATMULS_PER_GROUP
+            group = matmuls[first : first + MATMULS_PER_GROUP]
+            for m in group:
+                matmul(m)
+            ops.extend(late)
+            late.clear()
+            late.extend(("sum",) + m[1:4] + (0,) for m in group if m[0] == "mx" and m[4] == PASSES - 1)
         ops.append(("transpose",) + bank)
         ops.append(("copy",) + bank)
-        for ahead in banks[i + PERMUTE_AHEAD : i + PERMUTE_AHEAD + 1]:
-            permute(ahead)
-        now = list(late)
+        done.append(bank)
+        for nxt in banks[i + PERMUTE_AHEAD : i + PERMUTE_AHEAD + 1]:
+            permute(nxt)
+        ops.extend(late)
         late.clear()
         if kind == "h" and g == PASSES - 1:
             late.append(("quant_h", e, 0, 0, 0))
         if kind == "w" and sp == 1:
             late.append(("quant_w", e, j, g, 0))
-        ops.extend(now)
-        if i in unit_after and i < len(banks) - 1:
-            unit(*unit_after[i])
-            ops.extend(late)
-            late.clear()
-            late.append(("sum",) + unit_after[i] + (0,))
     ops.extend(late)
-    for u in units_after_all_banks():
-        unit(*u)
-        ops.append(("sum",) + u + (0,))
+    for m in matmuls[matmuls_among_banks() :]:
+        matmul(m)
+        if m[0] == "mx" and m[4] == PASSES - 1:
+            ops.append(("sum",) + m[1:4] + (0,))
     return ops
 
 
@@ -140,7 +163,7 @@ def tile_loralinearexpertswrapper_pb_kernel(tc, h, low_d, W_d, B_d, out):
                         w_pair = loads.tile([P, 2, D], BF16, name="w_pair%d%d%d" % (e, j, sp))
                         nc.sync.dma_start(out=w_pair[:], in_=rows[:, 2 * sp : 2 * sp + 2, :])
                         w_sb[e, j, sp] = w_pair[:]
-                if j == 0:
+                if j == (HALVES - 1 if e == 0 else 0):
                     low_sb[e] = loads.tile([P, TOK_TILES * R], BF16, name="low_sb%d" % e)
                     nc.sync.dma_start(out=low_sb[e][:], in_=low_d[e].rearrange("(p a) r -> p (a r)", a=TOK_TILES))
                     b_sb[e] = loads.tile([P, HALVES, SLOTS * R], BF16, name="b_sb%d" % e)
@@ -264,7 +287,7 @@ def tile_loralinearexpertswrapper_pb_kernel(tc, h, low_d, W_d, B_d, out):
             elif op == "mx":
                 e, j, a, g = step[1:]
                 if g == 0:
-                    if (e, j, a) in units_after_all_banks():
+                    if (e, j, a) in tiles_after_all_banks():
                         acc[e, j, a] = tp_pool.tile([P, N_TILE], F32, name="acc_late", tag="tp")
                     else:
                         acc[e, j, a] = acc_pool.tile([P, N_TILE], F32, name="acc")

@@ -23,6 +23,7 @@ SLOTS = N_TILE // P
 WHOLE_HALVES_FROM = 2
 LAST_PIECES = 2
 FIRST_GROUP_AFTER = 12
+FIRST_RUNS = (2, 4)
 BANKS_PER_RUN = 3
 MATMULS_PER_GROUP = 3
 PERMUTE_AHEAD = 4
@@ -74,9 +75,17 @@ def all_matmuls():
     ]
 
 
+def group_starts():
+    starts = [FIRST_GROUP_AFTER]
+    for n in FIRST_RUNS:
+        starts.append(starts[-1] + n)
+    while starts[-1] + BANKS_PER_RUN < len(all_banks()):
+        starts.append(starts[-1] + BANKS_PER_RUN)
+    return starts
+
+
 def matmuls_among_banks():
-    runs = -(-(len(all_banks()) - FIRST_GROUP_AFTER) // BANKS_PER_RUN)
-    return runs * MATMULS_PER_GROUP
+    return len(group_starts()) * MATMULS_PER_GROUP
 
 
 def tiles_after_all_banks():
@@ -104,9 +113,8 @@ def schedule():
         permute(bank)
     for i, bank in enumerate(banks):
         kind, e, j, g, sp = bank
-        ahead = i - FIRST_GROUP_AFTER
-        if ahead >= 0 and ahead % BANKS_PER_RUN == 0:
-            first = ahead // BANKS_PER_RUN * MATMULS_PER_GROUP
+        if i in group_starts():
+            first = group_starts().index(i) * MATMULS_PER_GROUP
             group = matmuls[first : first + MATMULS_PER_GROUP]
             for m in group:
                 matmul(m)

from contextlib import ExitStack

import concourse.masks as masks
import concourse.mybir as mybir

E, T, H, D, R = 4, 256, 1024, 1024, 128
FLOPS = 2 * E * T * H * (D + R)

F32 = mybir.dt.float32
BF16 = mybir.dt.bfloat16
U32 = mybir.dt.uint32
U8 = mybir.dt.uint8
E5M2X4 = mybir.dt.float8_e5m2_x4

P = 128
K_PASS = 512
PASSES = D // K_PASS
N_TILE = 512
HALVES = H // N_TILE
TOK_TILES = T // P
SLOTS = N_TILE // P

WHOLE_HALVES_FROM = 2
LAST_PIECES = 2
FIRST_GROUP_AFTER = 12
FIRST_RUNS = (2, 4)
BANKS_PER_RUN = 3
MATMULS_PER_GROUP = 3
PERMUTE_AHEAD = 4
VECTOR_BANKS_FIRST = (1, 3, 5, 8)
VECTOR_BANKS = (8,)


def bank_list(e):
    banks = [("h", e, 0, g, 0) for g in range(PASSES)]
    for j in range(HALVES):
        banks += [("w", e, j, g, sp) for sp in range(2) for g in range(PASSES)]
        banks.append(("b", e, j, 0, 0))
    if e == 0:
        banks = [b for b in banks if b[0] != "b"] + [b for b in banks if b[0] == "b"]
    return banks


def load_of(bank):
    kind, e, j, g, sp = bank
    return (kind, e, j, 0, sp)


def is_permuted(bank):
    kind, e, j, g, sp = bank
    return kind == "w" and e > 0 and (j, sp) != (1, 0)


def on_vector(bank):
    e = bank[1]
    return bank[0] != "b" and bank_list(e).index(bank) in (VECTOR_BANKS if e > 0 else VECTOR_BANKS_FIRST)


def all_banks():
    return [b for e in range(E) for b in bank_list(e)]


def matmuls_of_tile(e, j, a):
    steps = [("delta", e, j, a, 0), ("mx", e, j, a, 0), ("mx", e, j, a, 1)]
    return steps[1:] + steps[:1] if (e, j, a) == (0, 0, 0) else steps


def all_matmuls():
    return [
        step
        for e in range(E)
        for j in range(HALVES)
        for a in range(TOK_TILES)
        for step in matmuls_of_tile(e, j, a)
    ]


def group_starts():
    starts = [FIRST_GROUP_AFTER]
    for n in FIRST_RUNS:
        starts.append(starts[-1] + n)
    while starts[-1] + BANKS_PER_RUN < len(all_banks()):
        starts.append(starts[-1] + BANKS_PER_RUN)
    return starts


def matmuls_among_banks():
    return len(group_starts()) * MATMULS_PER_GROUP


def tiles_after_all_banks():
    return [m[1:4] for m in all_matmuls()[matmuls_among_banks() :] if m[0] == "mx" and m[4] == 0]


def schedule():
    banks = all_banks()
    matmuls = all_matmuls()
    ops = []
    late = []
    done = []

    def matmul(m):
        ops.append(m)
        if m[0] == "delta":
            ops.append(("delta_out",) + m[1:])

    def permute(bank):
        step = ("permute",) + load_of(bank)
        if is_permuted(bank) and step not in ops:
            ops.append(step)

    for bank in banks[:PERMUTE_AHEAD]:
        permute(bank)
    for i, bank in enumerate(banks):
        kind, e, j, g, sp = bank
        if i in group_starts():
            first = group_starts().index(i) * MATMULS_PER_GROUP
            group = matmuls[first : first + MATMULS_PER_GROUP]
            for m in group:
                matmul(m)
            ops.extend(late)
            late.clear()
            late.extend(("sum",) + m[1:4] + (0,) for m in group if m[0] == "mx" and m[4] == PASSES - 1)
        ops.append(("transpose",) + bank)
        ops.append(("copy",) + bank)
        done.append(bank)
        for nxt in banks[i + PERMUTE_AHEAD : i + PERMUTE_AHEAD + 1]:
            permute(nxt)
        ops.extend(late)
        late.clear()
        if kind == "h" and g == PASSES - 1:
            late.append(("quant_h", e, 0, 0, 0))
        if kind == "w" and sp == 1:
            late.append(("quant_w", e, j, g, 0))
    ops.extend(late)
    for m in matmuls[matmuls_among_banks() :]:
        matmul(m)
        if m[0] == "mx" and m[4] == PASSES - 1:
            ops.append(("sum",) + m[1:4] + (0,))
    return ops


def tile_loralinearexpertswrapper_pb_kernel(tc, h, low_d, W_d, B_d, out):
    nc = tc.nc
    out_v = out.rearrange("(e p a) n -> e p a n", e=E, a=TOK_TILES)

    with ExitStack() as ctx:
        ctx.enter_context(tc.manual_schedule())
        const = ctx.enter_context(tc.tile_pool(name="const", bufs=1))
        loads = ctx.enter_context(tc.tile_pool(name="loads", bufs=1))
        work = ctx.enter_context(tc.tile_pool(name="work", bufs=3))
        results = ctx.enter_context(tc.tile_pool(name="results", bufs=4))
        tp_pool = ctx.enter_context(tc.psum_pool(name="tp", bufs=4))
        acc_pool = ctx.enter_context(tc.psum_pool(name="acc", bufs=2))
        dl_pool = ctx.enter_context(tc.psum_pool(name="dl", bufs=2))

        h_sb, w_sb, b_sb, low_sb = {}, {}, {}, {}
        for e in range(E):
            h_pair = loads.tile([P, TOK_TILES, D], BF16, name="h_pair%d" % e)
            nc.sync.dma_start(out=h_pair[:], in_=h[e].rearrange("(p a) k -> p a k", a=TOK_TILES))
            h_sb[e] = h_pair[:]
            for j in range(HALVES):
                rows = W_d[e, j * N_TILE : (j + 1) * N_TILE, :].rearrange("(p s) k -> p s k", s=SLOTS)
                if e >= WHOLE_HALVES_FROM:
                    w_half = loads.tile([P, SLOTS, D], BF16, name="w_half%d%d" % (e, j))
                    nc.sync.dma_start(out=w_half[:], in_=rows)
                    for sp in range(2):
                        w_sb[e, j, sp] = w_half[:, 2 * sp : 2 * sp + 2, :]
                else:
                    for sp in range(2):
                        w_pair = loads.tile([P, 2, D], BF16, name="w_pair%d%d%d" % (e, j, sp))
                        nc.sync.dma_start(out=w_pair[:], in_=rows[:, 2 * sp : 2 * sp + 2, :])
                        w_sb[e, j, sp] = w_pair[:]
                if j == (HALVES - 1 if e == 0 else 0):
                    low_sb[e] = loads.tile([P, TOK_TILES * R], BF16, name="low_sb%d" % e)
                    nc.sync.dma_start(out=low_sb[e][:], in_=low_d[e].rearrange("(p a) r -> p (a r)", a=TOK_TILES))
                    b_sb[e] = loads.tile([P, HALVES, SLOTS * R], BF16, name="b_sb%d" % e)
                    nc.sync.dma_start(
                        out=b_sb[e][:], in_=B_d[e].rearrange("(j p s) r -> p j (s r)", j=HALVES, s=SLOTS)
                    )

        ident_f32 = const.tile([P, P], F32, name="ident_f32")
        masks.make_identity(nc, ident_f32[:])
        ident_bf16 = const.tile([P, P], BF16, name="ident_bf16")
        masks.make_identity(nc, ident_bf16[:])

        warm = const.tile([P, 8], F32, name="warm")
        nc.vector.memset(warm[:], 0.0)
        warm_out = const.tile([P, 8], F32, name="warm_out")
        nc.scalar.activation(out=warm_out[:], in_=warm[:], func=mybir.ActivationFunctionType.Copy, scale=2.0)

        tp, ordered, grouped, codes, scales, plain_t, acc, dl, dl_sb, res_all = {}, {}, {}, {}, {}, {}, {}, {}, {}, {}

        def transpose_words(dst, bank):
            kind, e, j, g, sp = bank
            for x in range(2):
                for u in range(2):
                    if is_permuted(bank):
                        words = ordered[load_of(bank)][:, PASSES * x + g, u, :]
                    else:
                        src = h_sb[e] if kind == "h" else w_sb[e, j, sp]
                        words = src[:, x, :].bitcast(F32)[:, 256 * g + u : 256 * (g + 1) : 2]
                    nc.tensor.transpose(dst[:, x, u, :], words, ident_f32[:])

        for step in schedule():
            op = step[0]
            if op == "permute":
                kind, e, j, g, sp = step[1:]
                src = h_sb[e] if kind == "h" else w_sb[e, j, sp]
                ordered[step[1:]] = work.tile([P, 2 * PASSES, 2, P], F32, name="ordered", bufs=5)
                nc.vector.tensor_copy(
                    out=ordered[step[1:]][:],
                    in_=src.rearrange("p x k -> p (x k)")
                    .bitcast(F32)
                    .rearrange("p (y q u) -> p y u q", y=2 * PASSES, u=2),
                )
            elif op == "transpose":
                kind, e, j, g, sp = step[1:]
                if kind == "b":
                    n = SLOTS + (TOK_TILES if j == 0 else 0)
                    t = tp_pool.tile([P, n, P], BF16, name="tp_b", tag="tp")
                    if j == 0:
                        for a in range(TOK_TILES):
                            nc.tensor.transpose(t[:, a, :], low_sb[e][:, a * R : (a + 1) * R], ident_bf16[:])
                    for s in range(SLOTS):
                        nc.tensor.transpose(
                            t[:, n - SLOTS + s, :], b_sb[e][:, j, s * R : (s + 1) * R], ident_bf16[:]
                        )
                else:
                    t = tp_pool.tile([P, 2, 2, P], F32, name="tp_w", tag="tp")
                    transpose_words(t, step[1:])
                tp[step[1:]] = t
            elif op == "copy":
                kind, e, j, g, sp = step[1:]
                t = tp[step[1:]]
                if kind == "b":
                    n = SLOTS + (TOK_TILES if j == 0 else 0)
                    plain_t[e, j] = work.tile([P, n * P], BF16, name="plain_t%d" % j, bufs=2)
                    nc.scalar.copy(out=plain_t[e, j][:], in_=t[:].rearrange("p n r -> p (n r)"))
                else:
                    if kind == "h":
                        if g == 0:
                            grouped["h", e, 0] = work.tile([P, PASSES, T, 2], F32, name="grouped_h", bufs=2, align_bytes=64)
                        dst = grouped["h", e, 0][:, g, :, :]
                    else:
                        if g == 0 and sp == 0:
                            grouped["w", e, j] = work.tile(
                                [P, PASSES, N_TILE, 2], F32, name="grouped_w", align_bytes=64
                            )
                        dst = grouped["w", e, j][:, g, 2 * P * sp : 2 * P * (sp + 1), :]
                    dst = dst.rearrange("p (x r) u -> p x r u", x=2)
                    src = t[:].rearrange("p x u r -> p x r u")
                    if on_vector(step[1:]):
                        nc.vector.tensor_copy(out=dst, in_=src)
                    else:
                        nc.scalar.copy(out=dst, in_=src)
            elif op == "quant_h":
                e = step[1]
                codes["h", e, 0] = work.tile([P, PASSES, T], U32, name="codes_h", bufs=2, align_bytes=64)
                scales["h", e, 0] = work.tile([P, PASSES, T], U8, name="scales_h", bufs=2, align_bytes=64)
                nc.vector.quantize_mx(
                    out=codes["h", e, 0][:].rearrange("p g c -> p (g c)").bitcast(E5M2X4),
                    scales=scales["h", e, 0][:].rearrange("p g c -> p (g c)"),
                    in_=grouped["h", e, 0][:].rearrange("p g c u -> p (g c u)").bitcast(BF16),
                )
            elif op == "quant_w":
                e, j, g = step[1:4]
                if g == 0:
                    codes["w", e, j] = work.tile([P, PASSES, N_TILE], U32, name="codes_w", align_bytes=64)
                    scales["w", e, j] = work.tile([P, PASSES, N_TILE], U8, name="scales_w", align_bytes=64)
                nc.vector.quantize_mx(
                    out=codes["w", e, j][:, g, :].bitcast(E5M2X4),
                    scales=scales["w", e, j][:, g, :],
                    in_=grouped["w", e, j][:, g, :, :].rearrange("p c u -> p (c u)").bitcast(BF16),
                )
            elif op == "delta":
                e, j, a = step[1:4]
                dl[e, j, a] = dl_pool.tile([P, N_TILE], F32, name="dl")
                nc.tensor.matmul(
                    dl[e, j, a][:],
                    lhsT=plain_t[e, 0][:, a * P : (a + 1) * P],
                    rhs=plain_t[e, 0][:, TOK_TILES * P :] if j == 0 else plain_t[e, 1][:],
                    start=True,
                    stop=True,
                )
            elif op == "delta_out":
                e, j, a = step[1:4]
                dl_sb[e, j, a] = work.tile([P, N_TILE], F32, name="dl_sb")
                nc.scalar.activation(
                    out=dl_sb[e, j, a][:].rearrange("p (r s) -> p r s", s=SLOTS),
                    in_=dl[e, j, a][:].rearrange("p (s r) -> p r s", s=SLOTS),
                    func=mybir.ActivationFunctionType.Copy,
                    scale=2.0,
                )
            elif op == "mx":
                e, j, a, g = step[1:]
                if g == 0:
                    if (e, j, a) in tiles_after_all_banks():
                        acc[e, j, a] = tp_pool.tile([P, N_TILE], F32, name="acc_late", tag="tp")
                    else:
                        acc[e, j, a] = acc_pool.tile([P, N_TILE], F32, name="acc")
                nc.tensor.matmul_mx(
                    out=acc[e, j, a][:],
                    lhsT=codes["h", e, 0][:, g, a * P : (a + 1) * P].bitcast(E5M2X4),
                    lhsT_scale=scales["h", e, 0][:, g, a * P : (a + 1) * P],
                    rhs=codes["w", e, j][:, g, :].bitcast(E5M2X4),
                    rhs_scale=scales["w", e, j][:, g, :],
                    start=(g == 0),
                    stop=(g == PASSES - 1),
                )
            elif op == "sum":
                e, j, a = step[1:4]
                if e < E - 1:
                    if (j, a) == (0, 0):
                        res_all[e] = results.tile([P, TOK_TILES, H], F32, name="res_all", bufs=E - 1)
                    nc.vector.tensor_tensor(
                        out=res_all[e][:, a, j * N_TILE : (j + 1) * N_TILE].rearrange("p (r s) -> p r s", s=SLOTS),
                        in0=acc[e, j, a][:].rearrange("p (s r) -> p r s", s=SLOTS),
                        in1=dl_sb[e, j, a][:].rearrange("p (r s) -> p r s", s=SLOTS),
                        op=mybir.AluOpType.add,
                    )
                    if (j, a) == (HALVES - 1, TOK_TILES - 1):
                        nc.sync.dma_start(out=out_v[e], in_=res_all[e][:])
                    continue
                res = results.tile([P, N_TILE], F32, name="res")
                pieces = LAST_PIECES if (e, j, a) == (E - 1, HALVES - 1, TOK_TILES - 1) else 1
                rows = P // pieces
                for c in range(pieces):
                    nc.vector.tensor_tensor(
                        out=res[:, c * rows * SLOTS : (c + 1) * rows * SLOTS].rearrange("p (r s) -> p r s", s=SLOTS),
                        in0=acc[e, j, a][:].rearrange("p (s r) -> p r s", s=SLOTS)[:, c * rows : (c + 1) * rows, :],
                        in1=dl_sb[e, j, a][:, c * rows * SLOTS : (c + 1) * rows * SLOTS].rearrange("p (r s) -> p r s", s=SLOTS),
                        op=mybir.AluOpType.add,
                    )
                    nc.sync.dma_start(
                        out=out_v[e][:, a, j * N_TILE + c * rows * SLOTS : j * N_TILE + (c + 1) * rows * SLOTS],
                        in_=res[:, c * rows * SLOTS : (c + 1) * rows * SLOTS],
                    )
